import numpy as np
import ml_dtypes


def mxq(x, axis, fmt="e4m3"):
    dtype, down = {"e4m3": (ml_dtypes.float8_e4m3fn, 7), "e5m2": (ml_dtypes.float8_e5m2, 14)}[fmt]
    v = np.moveaxis(np.asarray(x, np.float32).astype(ml_dtypes.bfloat16).astype(np.float64), axis, -1)
    blocks = v.reshape(v.shape[:-1] + (-1, 32))
    amax = np.abs(blocks).max(-1, keepdims=True)
    byte = np.maximum(np.where(amax > 0, np.frexp(amax)[1] - 1 + 127, 0) - down, 1)
    scale = np.exp2(byte - 127.0)
    codes = (blocks / scale).astype(np.float32).astype(dtype).astype(np.float64)
    return np.moveaxis((codes * scale).reshape(v.shape), -1, axis)


WIDE = False


def mx_kscale(k):
    if not WIDE:
        return np.ones(k)
    levels = np.array([10, -10, 5, -5, 0])
    a = np.random.permutation(np.resize(levels, k // 512 * 4)).reshape(k // 512, 4)
    idx = np.arange(k)
    return np.exp2(a[idx // 512, idx % 128 // 32])


BF16 = ml_dtypes.bfloat16


def bf(x):
    return np.asarray(x, np.float32).astype(BF16)


def f64(x):
    return np.asarray(x).astype(np.float64)


C, P, B, D = 3, 512, 2, 64
N = C * P
ID = C // 2


def laplacian_with_self_loop(adj):
    a = adj + np.eye(adj.shape[0])
    d_inv_sqrt = 1.0 / np.sqrt(a.sum(axis=1))
    return d_inv_sqrt[:, None] * a * d_inv_sqrt[None, :]


def setup_inputs():
    s = mx_kscale(P)
    sp = s / s.min()
    r = np.exp2(np.random.uniform(-1.0, 1.0, N))
    adj = np.random.uniform(0.0, 1.0, (N, N)) * r[:, None] * np.tile(sp, C)[None, :]
    x = np.random.standard_normal((P, B * D)) * (0.15 * N * sp.mean() / np.sqrt(P / 3.0)) / sp[:, None]
    return {"globalAdj": bf(adj), "inputs": bf(x), "batch_size": B, "output_dim": D, "id": ID}


def reference(globalAdj, inputs, batch_size, output_dim, id):
    lap = laplacian_with_self_loop(f64(globalAdj))
    col = lap[:, id * P:(id + 1) * P]
    out = mxq(col, 1, "e4m3") @ mxq(f64(inputs), 0, "e4m3")
    out = out.reshape(N, batch_size, output_dim)
    return out.transpose(1, 0, 2)

@@ -1,0 +1,128 @@
+import concourse.mybir as mybir
+from concourse.masks import make_identity
+
+BF16 = mybir.dt.bfloat16
+F32 = mybir.dt.float32
+U32 = mybir.dt.uint32
+U8 = mybir.dt.uint8
+FP8X4 = mybir.dt.float8_e4m3fn_x4
+ALU = mybir.AluOpType
+ACT = mybir.ActivationFunctionType
+
+P = 128
+PACK = 4
+NODES = 1536
+CLIENT = P * PACK
+FEATURES = 128
+ROW_TILES = NODES // P
+HALF = NODES // 2
+
+FLOPS = 2 * NODES * CLIENT * FEATURES
+
+
+def tile_gcn_s_kernel(tc, globalAdj, inputs, batch_size, output_dim, client, out):
+    nc = tc.nc
+    assert batch_size * output_dim == FEATURES
+
+    own = list(range(PACK * client, PACK * client + PACK))
+    order = own + [r for r in range(ROW_TILES) if r not in own]
+
+    with tc.tile_pool(name="keep", bufs=1) as keep, tc.tile_pool(name="sums", bufs=ROW_TILES) as sums, tc.tile_pool(
+        name="work", bufs=4
+    ) as work, tc.psum_pool(name="turned", bufs=5) as turned_pool, tc.psum_pool(name="product", bufs=3) as product_pool:
+        x_raw = keep.tile([P, PACK, FEATURES], BF16)
+        nc.scalar.dma_start(out=x_raw[:], in_=inputs.rearrange("(t p) f -> p t f", p=P))
+        adj = []
+        for i in range(ROW_TILES):
+            rows = keep.tile([P, NODES], BF16, name="adj%d" % i)
+            nc.sync.dma_start(out=rows[:], in_=globalAdj[order[i] * P : (order[i] + 1) * P, :])
+            adj.append(rows)
+
+        ident = keep.tile([P, P], F32)
+        make_identity(nc, ident[:])
+        one = keep.tile([P, 1], F32)
+        nc.vector.memset(one[:], 1.0)
+        warm = keep.tile([P, 1], F32)
+        nc.scalar.activation(out=warm[:], in_=one[:], func=ACT.Sqrt)
+
+        x_grouped = keep.tile([P, FEATURES, PACK], BF16, align_bytes=64)
+        nc.vector.tensor_copy(out=x_grouped[:], in_=x_raw[:].rearrange("p t f -> p f t"))
+        x_codes = keep.tile([P, FEATURES], U32, align_bytes=64)
+        x_scales = keep.tile([P, FEATURES], U8, align_bytes=64)
+        nc.vector.quantize_mx(
+            out=x_codes[:].bitcast(FP8X4), scales=x_scales[:], in_=x_grouped[:].rearrange("p f t -> p (f t)")
+        )
+
+        degree = keep.tile([P, ROW_TILES, 8], F32)
+        root = keep.tile([P, ROW_TILES], F32)
+        dinv = keep.tile([P, ROW_TILES], F32)
+
+        turned = {}
+
+        def front(i):
+            if i % 3 == 2:
+                unused = sums.tile([P, NODES], BF16, name="unused_s")
+                nc.scalar.activation(out=unused[:], in_=adj[i][:], func=ACT.Copy, accum_out=degree[:, i, 0:1])
+            else:
+                unused = sums.tile([P, HALF], F32, name="unused_v")
+                nc.vector.scalar_tensor_tensor(
+                    out=unused[:],
+                    in0=adj[i][:, 0:HALF],
+                    scalar=1.0,
+                    in1=adj[i][:, HALF:NODES],
+                    op0=ALU.mult,
+                    op1=ALU.add,
+                    accum_out=degree[:, i, 0:1],
+                )
+            nc.scalar.activation(out=root[:, i : i + 1], in_=degree[:, i, 0:1], func=ACT.Sqrt, bias=1.0)
+            nc.vector.reciprocal(out=dinv[:, i : i + 1], in_=root[:, i : i + 1])
+            scaled = work.tile([P, CLIENT], F32)
+            nc.scalar.activation(
+                out=scaled[:], in_=adj[i][:, client * CLIENT : (client + 1) * CLIENT], func=ACT.Copy, scale=dinv[:, i : i + 1]
+            )
+            if i < PACK:
+                block = scaled[:, i * P : (i + 1) * P]
+                nc.vector.scalar_tensor_tensor(
+                    out=block, in0=ident[:], scalar=dinv[:, i : i + 1], in1=block, op0=ALU.mult, op1=ALU.add
+                )
+            bank = turned_pool.tile([P, PACK, P], F32)
+            for t in range(PACK):
+                nc.tensor.transpose(bank[:, t, :], scaled[:, t * P : (t + 1) * P], ident[:])
+            turned[i] = bank
+
+        def back(i):
+            grouped = work.tile([P, P, PACK], BF16, align_bytes=64)
+            nc.vector.tensor_tensor(
+                out=grouped[:],
+                in0=turned[i][:].rearrange("p t n -> p n t"),
+                in1=dinv[:, 0:PACK].unsqueeze(1).to_broadcast([P, P, PACK]),
+                op=ALU.mult,
+            )
+            codes = work.tile([P, P], U32, align_bytes=64)
+            scales = work.tile([P, P], U8, align_bytes=64)
+            nc.vector.quantize_mx(
+                out=codes[:].bitcast(FP8X4), scales=scales[:], in_=grouped[:].rearrange("p n t -> p (n t)")
+            )
+            product = product_pool.tile([P, FEATURES], F32)
+            nc.tensor.matmul_mx(
+                out=product[:],
+                lhsT=codes[:].bitcast(FP8X4),
+                lhsT_scale=scales[:],
+                rhs=x_codes[:].bitcast(FP8X4),
+                rhs_scale=x_scales[:],
+                start=True,
+                stop=True,
+            )
+            y = work.tile([P, FEATURES], F32)
+            nc.scalar.copy(out=y[:], in_=product[:])
+            r = order[i]
+            nc.sync.dma_start(
+                out=out[:, r * P : (r + 1) * P, :].rearrange("b n f -> n b f"),
+                in_=y[:].rearrange("n (b f) -> n b f", b=batch_size),
+            )
+
+        for i in range(ROW_TILES + PACK):
+            if i < ROW_TILES:
+                front(i)
+            if i >= PACK:
+                back(i - PACK)

@@ -29,38 +29,44 @@ def tile_gcn_s_kernel(tc, globalAdj, inputs, batch_size, output_dim, client, out
 
     with tc.tile_pool(name="keep", bufs=1) as keep, tc.tile_pool(name="sums", bufs=ROW_TILES) as sums, tc.tile_pool(
         name="work", bufs=4
-    ) as work, tc.psum_pool(name="turned", bufs=5) as turned_pool, tc.psum_pool(name="product", bufs=3) as product_pool:
+    ) as work, tc.psum_pool(name="turned", bufs=4) as turned_pool, tc.psum_pool(
+        name="product", bufs=4
+    ) as product_pool, tc.manual_schedule():
         x_raw = keep.tile([P, PACK, FEATURES], BF16)
-        nc.scalar.dma_start(out=x_raw[:], in_=inputs.rearrange("(t p) f -> p t f", p=P))
         adj = []
         for i in range(ROW_TILES):
             rows = keep.tile([P, NODES], BF16, name="adj%d" % i)
             nc.sync.dma_start(out=rows[:], in_=globalAdj[order[i] * P : (order[i] + 1) * P, :])
             adj.append(rows)
+            if i == PACK - 1:
+                nc.sync.dma_start(out=x_raw[:], in_=inputs.rearrange("(t p) f -> p t f", p=P))
 
         ident = keep.tile([P, P], F32)
         make_identity(nc, ident[:])
-        one = keep.tile([P, 1], F32)
-        nc.vector.memset(one[:], 1.0)
-        warm = keep.tile([P, 1], F32)
-        nc.scalar.activation(out=warm[:], in_=one[:], func=ACT.Sqrt)
+
+        minus_half = keep.tile([P, 1], F32)
+        nc.gpsimd.memset(minus_half[:], -0.5)
 
         x_grouped = keep.tile([P, FEATURES, PACK], BF16, align_bytes=64)
-        nc.vector.tensor_copy(out=x_grouped[:], in_=x_raw[:].rearrange("p t f -> p f t"))
         x_codes = keep.tile([P, FEATURES], U32, align_bytes=64)
         x_scales = keep.tile([P, FEATURES], U8, align_bytes=64)
-        nc.vector.quantize_mx(
-            out=x_codes[:].bitcast(FP8X4), scales=x_scales[:], in_=x_grouped[:].rearrange("p f t -> p (f t)")
-        )
+
+        def quantise_inputs():
+            nc.vector.tensor_copy(out=x_grouped[:], in_=x_raw[:].rearrange("p t f -> p f t"))
+            nc.vector.quantize_mx(
+                out=x_codes[:].bitcast(FP8X4), scales=x_scales[:], in_=x_grouped[:].rearrange("p f t -> p (f t)")
+            )
 
         degree = keep.tile([P, ROW_TILES, 8], F32)
-        root = keep.tile([P, ROW_TILES], F32)
         dinv = keep.tile([P, ROW_TILES], F32)
 
+        scaled = {}
         turned = {}
+        grouped = {}
+        product = {}
 
-        def front(i):
-            if i % 3 == 2:
+        def row_sum(i):
+            if PACK <= i < ROW_TILES - 2 and i % 2 == 0:
                 unused = sums.tile([P, NODES], BF16, name="unused_s")
                 nc.scalar.activation(out=unused[:], in_=adj[i][:], func=ACT.Copy, accum_out=degree[:, i, 0:1])
             else:
@@ -74,38 +80,50 @@ def tile_gcn_s_kernel(tc, globalAdj, inputs, batch_size, output_dim, client, out
                     op1=ALU.add,
                     accum_out=degree[:, i, 0:1],
                 )
-            nc.scalar.activation(out=root[:, i : i + 1], in_=degree[:, i, 0:1], func=ACT.Sqrt, bias=1.0)
-            nc.vector.reciprocal(out=dinv[:, i : i + 1], in_=root[:, i : i + 1])
-            scaled = work.tile([P, CLIENT], F32)
-            nc.scalar.activation(
-                out=scaled[:], in_=adj[i][:, client * CLIENT : (client + 1) * CLIENT], func=ACT.Copy, scale=dinv[:, i : i + 1]
+
+        def inverse_root(i):
+            nc.gpsimd.tensor_scalar(
+                out=degree[:, i, 1:2], in0=degree[:, i, 0:1], scalar1=1.0, scalar2=1.0, op0=ALU.mult, op1=ALU.add
             )
+            nc.gpsimd.tensor_tensor(out=dinv[:, i : i + 1], in0=degree[:, i, 1:2], in1=minus_half[:], op=ALU.pow)
+
+        def scale_rows(i):
+            scaled[i] = work.tile([P, CLIENT], F32, name="scaled")
+            nc.scalar.activation(
+                out=scaled[i][:],
+                in_=adj[i][:, client * CLIENT : (client + 1) * CLIENT],
+                func=ACT.Copy,
+                scale=dinv[:, i : i + 1],
+            )
+
+        def turn(i):
             if i < PACK:
-                block = scaled[:, i * P : (i + 1) * P]
+                block = scaled[i][:, i * P : (i + 1) * P]
                 nc.vector.scalar_tensor_tensor(
                     out=block, in0=ident[:], scalar=dinv[:, i : i + 1], in1=block, op0=ALU.mult, op1=ALU.add
                 )
-            bank = turned_pool.tile([P, PACK, P], F32)
+            turned[i] = turned_pool.tile([P, PACK, P], F32, name="turned")
             for t in range(PACK):
-                nc.tensor.transpose(bank[:, t, :], scaled[:, t * P : (t + 1) * P], ident[:])
-            turned[i] = bank
+                nc.tensor.transpose(turned[i][:, t, :], scaled[i][:, t * P : (t + 1) * P], ident[:])
 
-        def back(i):
-            grouped = work.tile([P, P, PACK], BF16, align_bytes=64)
+        def scale_columns(i):
+            grouped[i] = work.tile([P, P, PACK], BF16, name="grouped", align_bytes=64)
             nc.vector.tensor_tensor(
-                out=grouped[:],
+                out=grouped[i][:],
                 in0=turned[i][:].rearrange("p t n -> p n t"),
                 in1=dinv[:, 0:PACK].unsqueeze(1).to_broadcast([P, P, PACK]),
                 op=ALU.mult,
             )
+
+        def quantise_and_multiply(i):
             codes = work.tile([P, P], U32, align_bytes=64)
             scales = work.tile([P, P], U8, align_bytes=64)
             nc.vector.quantize_mx(
-                out=codes[:].bitcast(FP8X4), scales=scales[:], in_=grouped[:].rearrange("p n t -> p (n t)")
+                out=codes[:].bitcast(FP8X4), scales=scales[:], in_=grouped[i][:].rearrange("p n t -> p (n t)")
             )
-            product = product_pool.tile([P, FEATURES], F32)
+            product[i] = product_pool.tile([P, FEATURES], F32, name="product")
             nc.tensor.matmul_mx(
-                out=product[:],
+                out=product[i][:],
                 lhsT=codes[:].bitcast(FP8X4),
                 lhsT_scale=scales[:],
                 rhs=x_codes[:].bitcast(FP8X4),
@@ -113,16 +131,32 @@ def tile_gcn_s_kernel(tc, globalAdj, inputs, batch_size, output_dim, client, out
                 start=True,
                 stop=True,
             )
+
+        def store(i):
             y = work.tile([P, FEATURES], F32)
-            nc.scalar.copy(out=y[:], in_=product[:])
+            nc.scalar.copy(out=y[:], in_=product[i][:])
             r = order[i]
             nc.sync.dma_start(
                 out=out[:, r * P : (r + 1) * P, :].rearrange("b n f -> n b f"),
                 in_=y[:].rearrange("n (b f) -> n b f", b=batch_size),
             )
 
-        for i in range(ROW_TILES + PACK):
-            if i < ROW_TILES:
-                front(i)
-            if i >= PACK:
-                back(i - PACK)
+        def in_range(i):
+            return 0 <= i < ROW_TILES
+
+        for step in range(ROW_TILES + 7):
+            if in_range(step - 7):
+                store(step - 7)
+            if in_range(step - 2):
+                scale_rows(step - 2)
+            if in_range(step):
+                row_sum(step)
+                inverse_root(step)
+            if step == PACK:
+                quantise_inputs()
+            if in_range(step - 3):
+                turn(step - 3)
+            if in_range(step - 5):
+                quantise_and_multiply(step - 5)
+            if in_range(step - 4):
+                scale_columns(step - 4)

@@ -44,8 +44,11 @@ def tile_gcn_s_kernel(tc, globalAdj, inputs, batch_size, output_dim, client, out
         ident = keep.tile([P, P], F32)
         make_identity(nc, ident[:])
 
-        minus_half = keep.tile([P, 1], F32)
-        nc.gpsimd.memset(minus_half[:], -0.5)
+        one = keep.tile([P, 1], F32)
+        nc.vector.memset(one[:], 1.0)
+        warm = keep.tile([P, 1], F32)
+        nc.scalar.activation(out=warm[:], in_=one[:], func=ACT.Sqrt)
+        roots = keep.tile([P, ROW_TILES], F32)
 
         x_grouped = keep.tile([P, FEATURES, PACK], BF16, align_bytes=64)
         x_codes = keep.tile([P, FEATURES], U32, align_bytes=64)
@@ -81,11 +84,11 @@ def tile_gcn_s_kernel(tc, globalAdj, inputs, batch_size, output_dim, client, out
                     accum_out=degree[:, i, 0:1],
                 )
 
+        def root(i):
+            nc.scalar.activation(out=roots[:, i : i + 1], in_=degree[:, i, 0:1], func=ACT.Sqrt, bias=1.0)
+
         def inverse_root(i):
-            nc.gpsimd.tensor_scalar(
-                out=degree[:, i, 1:2], in0=degree[:, i, 0:1], scalar1=1.0, scalar2=1.0, op0=ALU.mult, op1=ALU.add
-            )
-            nc.gpsimd.tensor_tensor(out=dinv[:, i : i + 1], in0=degree[:, i, 1:2], in1=minus_half[:], op=ALU.pow)
+            nc.vector.reciprocal(out=dinv[:, i : i + 1], in_=roots[:, i : i + 1])
 
         def scale_rows(i):
             scaled[i] = work.tile([P, CLIENT], F32, name="scaled")
@@ -147,13 +150,16 @@ def tile_gcn_s_kernel(tc, globalAdj, inputs, batch_size, output_dim, client, out
         for step in range(ROW_TILES + 7):
             if in_range(step - 7):
                 store(step - 7)
+            if in_range(step - 1):
+                root(step - 1)
             if in_range(step - 2):
                 scale_rows(step - 2)
             if in_range(step):
                 row_sum(step)
-                inverse_root(step)
             if step == PACK:
                 quantise_inputs()
+            if in_range(step - 1):
+                inverse_root(step - 1)
             if in_range(step - 3):
                 turn(step - 3)
             if in_range(step - 5):

import concourse.mybir as mybir
from concourse.masks import make_identity

BF16 = mybir.dt.bfloat16
F32 = mybir.dt.float32
U32 = mybir.dt.uint32
U8 = mybir.dt.uint8
FP8X4 = mybir.dt.float8_e4m3fn_x4
ALU = mybir.AluOpType
ACT = mybir.ActivationFunctionType

P = 128
PACK = 4
NODES = 1536
CLIENT = P * PACK
FEATURES = 128
ROW_TILES = NODES // P
HALF = NODES // 2

FLOPS = 2 * NODES * CLIENT * FEATURES


def tile_gcn_s_kernel(tc, globalAdj, inputs, batch_size, output_dim, client, out):
    nc = tc.nc
    assert batch_size * output_dim == FEATURES

    own = list(range(PACK * client, PACK * client + PACK))
    order = own + [r for r in range(ROW_TILES) if r not in own]

    with tc.tile_pool(name="keep", bufs=1) as keep, tc.tile_pool(name="sums", bufs=ROW_TILES) as sums, tc.tile_pool(
        name="work", bufs=4
    ) as work, tc.psum_pool(name="turned", bufs=4) as turned_pool, tc.psum_pool(
        name="product", bufs=4
    ) as product_pool, tc.manual_schedule():
        x_raw = keep.tile([P, PACK, FEATURES], BF16)
        adj = []
        for i in range(ROW_TILES):
            rows = keep.tile([P, NODES], BF16, name="adj%d" % i)
            nc.sync.dma_start(out=rows[:], in_=globalAdj[order[i] * P : (order[i] + 1) * P, :])
            adj.append(rows)
            if i == PACK - 1:
                nc.sync.dma_start(out=x_raw[:], in_=inputs.rearrange("(t p) f -> p t f", p=P))

        ident = keep.tile([P, P], F32)
        make_identity(nc, ident[:])

        one = keep.tile([P, 1], F32)
        nc.vector.memset(one[:], 1.0)
        warm = keep.tile([P, 1], F32)
        nc.scalar.activation(out=warm[:], in_=one[:], func=ACT.Sqrt)
        roots = keep.tile([P, ROW_TILES], F32)

        x_grouped = keep.tile([P, FEATURES, PACK], BF16, align_bytes=64)
        x_codes = keep.tile([P, FEATURES], U32, align_bytes=64)
        x_scales = keep.tile([P, FEATURES], U8, align_bytes=64)

        def quantise_inputs():
            nc.vector.tensor_copy(out=x_grouped[:], in_=x_raw[:].rearrange("p t f -> p f t"))
            nc.vector.quantize_mx(
                out=x_codes[:].bitcast(FP8X4), scales=x_scales[:], in_=x_grouped[:].rearrange("p f t -> p (f t)")
            )

        degree = keep.tile([P, ROW_TILES, 8], F32)
        dinv = keep.tile([P, ROW_TILES], F32)

        scaled = {}
        turned = {}
        grouped = {}
        product = {}

        def row_sum(i):
            if PACK <= i < ROW_TILES - 2 and i % 2 == 0:
                unused = sums.tile([P, NODES], BF16, name="unused_s")
                nc.scalar.activation(out=unused[:], in_=adj[i][:], func=ACT.Copy, accum_out=degree[:, i, 0:1])
            else:
                unused = sums.tile([P, HALF], F32, name="unused_v")
                nc.vector.scalar_tensor_tensor(
                    out=unused[:],
                    in0=adj[i][:, 0:HALF],
                    scalar=1.0,
                    in1=adj[i][:, HALF:NODES],
                    op0=ALU.mult,
                    op1=ALU.add,
                    accum_out=degree[:, i, 0:1],
                )

        def root(i):
            nc.scalar.activation(out=roots[:, i : i + 1], in_=degree[:, i, 0:1], func=ACT.Sqrt, bias=1.0)

        def inverse_root(i):
            nc.vector.reciprocal(out=dinv[:, i : i + 1], in_=roots[:, i : i + 1])

        def scale_rows(i):
            scaled[i] = work.tile([P, CLIENT], F32, name="scaled")
            nc.scalar.activation(
                out=scaled[i][:],
                in_=adj[i][:, client * CLIENT : (client + 1) * CLIENT],
                func=ACT.Copy,
                scale=dinv[:, i : i + 1],
            )

        def turn(i):
            if i < PACK:
                block = scaled[i][:, i * P : (i + 1) * P]
                nc.vector.scalar_tensor_tensor(
                    out=block, in0=ident[:], scalar=dinv[:, i : i + 1], in1=block, op0=ALU.mult, op1=ALU.add
                )
            turned[i] = turned_pool.tile([P, PACK, P], F32, name="turned")
            for t in range(PACK):
                nc.tensor.transpose(turned[i][:, t, :], scaled[i][:, t * P : (t + 1) * P], ident[:])

        def scale_columns(i):
            grouped[i] = work.tile([P, P, PACK], BF16, name="grouped", align_bytes=64)
            nc.vector.tensor_tensor(
                out=grouped[i][:],
                in0=turned[i][:].rearrange("p t n -> p n t"),
                in1=dinv[:, 0:PACK].unsqueeze(1).to_broadcast([P, P, PACK]),
                op=ALU.mult,
            )

        def quantise_and_multiply(i):
            codes = work.tile([P, P], U32, align_bytes=64)
            scales = work.tile([P, P], U8, align_bytes=64)
            nc.vector.quantize_mx(
                out=codes[:].bitcast(FP8X4), scales=scales[:], in_=grouped[i][:].rearrange("p n t -> p (n t)")
            )
            product[i] = product_pool.tile([P, FEATURES], F32, name="product")
            nc.tensor.matmul_mx(
                out=product[i][:],
                lhsT=codes[:].bitcast(FP8X4),
                lhsT_scale=scales[:],
                rhs=x_codes[:].bitcast(FP8X4),
                rhs_scale=x_scales[:],
                start=True,
                stop=True,
            )

        def store(i):
            y = work.tile([P, FEATURES], F32)
            nc.scalar.copy(out=y[:], in_=product[i][:])
            r = order[i]
            nc.sync.dma_start(
                out=out[:, r * P : (r + 1) * P, :].rearrange("b n f -> n b f"),
                in_=y[:].rearrange("n (b f) -> n b f", b=batch_size),
            )

        def in_range(i):
            return 0 <= i < ROW_TILES

        for step in range(ROW_TILES + 7):
            if in_range(step - 7):
                store(step - 7)
            if in_range(step - 1):
                root(step - 1)
            if in_range(step - 2):
                scale_rows(step - 2)
            if in_range(step):
                row_sum(step)
            if step == PACK:
                quantise_inputs()
            if in_range(step - 1):
                inverse_root(step - 1)
            if in_range(step - 3):
                turn(step - 3)
            if in_range(step - 5):
                quantise_and_multiply(step - 5)
            if in_range(step - 4):
                scale_columns(step - 4)
